import numpy as np
import ml_dtypes


def mxq(x, axis, fmt="e4m3"):
    dtype, down = {"e4m3": (ml_dtypes.float8_e4m3fn, 7), "e5m2": (ml_dtypes.float8_e5m2, 14)}[fmt]
    v = np.moveaxis(np.asarray(x, np.float32).astype(ml_dtypes.bfloat16).astype(np.float64), axis, -1)
    blocks = v.reshape(v.shape[:-1] + (-1, 32))
    amax = np.abs(blocks).max(-1, keepdims=True)
    byte = np.maximum(np.where(amax > 0, np.frexp(amax)[1] - 1 + 127, 0) - down, 1)
    scale = np.exp2(byte - 127.0)
    codes = (blocks / scale).astype(np.float32).astype(dtype).astype(np.float64)
    return np.moveaxis((codes * scale).reshape(v.shape), -1, axis)


WIDE = False


def mx_kscale(k):
    if not WIDE:
        return np.ones(k)
    levels = np.array([10, -10, 5, -5, 0])
    if k % 512:
        return np.exp2(np.random.permutation(np.resize(levels, k // 32))).repeat(32)
    a = np.empty((k // 512, 16))
    for p in range(k // 512):
        a[p, :8] = np.random.permutation(np.resize(levels, 8))
        for g in range(8):
            far = levels[np.abs(levels - a[p, g]) >= 10]
            a[p, g + 8] = far[np.random.randint(len(far))]
    return np.exp2(a.ravel()).repeat(32)


BF16 = ml_dtypes.bfloat16


def bf(x):
    return np.asarray(x, np.float32).astype(BF16)


def f64(x):
    return np.asarray(x).astype(np.float64)


B, T, S, Dt, Df = 8, 1024, 256, 512, 512
EPS = 1e-6


def rmsnorm(x, w):
    return x * (1.0 / np.sqrt(np.mean(x * x, axis=-1, keepdims=True) + EPS)) * w


def setup_inputs():
    s = mx_kscale(Dt)
    t = mx_kscale(Df)
    return {"text": bf(np.random.standard_normal((B, T, Dt)) * s),
            "Wq_w": bf(np.random.standard_normal((Df, Dt)) / np.sqrt(Dt) / s[None, :]),
            "Wq_b": bf(np.random.standard_normal(Df) * 0.3),
            "qn_w": bf((1.0 + 0.1 * np.random.standard_normal(Df)) * t),
            "k_norm": bf(np.random.standard_normal((B, S, Df)) / t)}


def reference(text, Wq_w, Wq_b, qn_w, k_norm):
    q = (mxq(f64(text), 2, "e4m3") @ mxq(f64(Wq_w), 1, "e4m3").T) + f64(Wq_b)
    q = rmsnorm(q, f64(qn_w))
    scale = 1.0 / np.sqrt(Df)
    return (mxq(q, 2, "e4m3") @ mxq(f64(k_norm), 2, "e4m3").transpose(0, 2, 1)) * scale

@@ -1,0 +1,277 @@
+from contextlib import ExitStack
+import math
+
+import concourse.mybir as mybir
+from concourse.masks import make_identity
+
+F32 = mybir.dt.float32
+BF16 = mybir.dt.bfloat16
+U32 = mybir.dt.uint32
+U8 = mybir.dt.uint8
+FP8X4 = mybir.dt.float8_e4m3fn_x4
+ACT = mybir.ActivationFunctionType
+ALU = mybir.AluOpType
+
+P = 128
+PACK = 4
+BATCHES = 8
+TOKENS = 1024
+KEYS = 256
+D = 512
+EPS = 1e-6
+
+CHUNKS = D // P
+TILES_PER_BATCH = TOKENS // P
+KEY_TILES = KEYS // P
+BLOCK_TILES = 4
+BLOCK = BLOCK_TILES * P
+BLOCKS_PER_BATCH = TOKENS // BLOCK
+N_BLOCKS = BATCHES * BLOCKS_PER_BATCH
+PAIR = 2
+RUN = 4
+
+FLOPS = 2 * BATCHES * TOKENS * D * D + 2 * BATCHES * TOKENS * D * KEYS
+
+
+def tile_crossattention_pb_t_kernel(tc, text, Wq_w, Wq_b, qn_w, k_norm, out):
+    nc = tc.nc
+    with ExitStack() as ctx:
+        ctx.enter_context(tc.manual_schedule())
+        const = ctx.enter_context(tc.tile_pool(name="const", bufs=1))
+        raw = ctx.enter_context(tc.tile_pool(name="raw", bufs=4))
+        stage = ctx.enter_context(tc.tile_pool(name="stage", bufs=2))
+        deep = ctx.enter_context(tc.tile_pool(name="deep", bufs=3))
+        deeper = ctx.enter_context(tc.tile_pool(name="deeper", bufs=4))
+        psum_ring = ctx.enter_context(tc.psum_pool(name="psum_ring", bufs=6))
+        psum_one = ctx.enter_context(tc.psum_pool(name="psum_one", bufs=1))
+
+        w_raw = const.tile([P, CHUNKS, D], BF16)
+        nc.sync.dma_start(
+            out=w_raw[:],
+            in_=Wq_w.rearrange("(p c) k -> p c k", c=CHUNKS),
+        )
+        bias_bf = const.tile([P, CHUNKS], BF16)
+        gain_bf = const.tile([P, CHUNKS], BF16)
+        nc.scalar.dma_start(
+            out=bias_bf[:],
+            in_=Wq_b.rearrange("(p c) -> p c", c=CHUNKS),
+        )
+        nc.scalar.dma_start(
+            out=gain_bf[:],
+            in_=qn_w.rearrange("(p c) -> p c", c=CHUNKS),
+        )
+        ident = const.tile([P, P], F32)
+        make_identity(nc, ident[:])
+        ones = const.tile([P, 1], F32)
+        nc.vector.memset(ones[:], 1.0)
+        eps = const.tile([P, 1], F32)
+        nc.vector.memset(eps[:], EPS)
+        bias = const.tile([P, CHUNKS], F32)
+        gain = const.tile([P, CHUNKS], F32)
+        gain_bias = const.tile([P, CHUNKS], F32)
+        nc.vector.tensor_copy(out=bias[:], in_=bias_bf[:])
+        nc.vector.tensor_copy(out=gain[:], in_=gain_bf[:])
+        nc.vector.tensor_tensor(out=gain_bias[:], in0=gain[:], in1=bias[:], op=ALU.mult)
+
+        turned_operands = []
+
+        def quantise(operand):
+            grouped, codes, scales = operand
+            nc.vector.quantize_mx(
+                out=codes.bitcast(FP8X4),
+                scales=scales,
+                in_=grouped[:].rearrange("p r t -> p (r t)"),
+            )
+
+        def transpose_and_quantise(rows, n_tiles, codes, scales):
+            words = rows.bitcast(F32)
+            grouped = deep.tile([P, n_tiles * P, PACK], BF16, align_bytes=64, tag="grouped%d" % n_tiles)
+            grouped_words = grouped[:].bitcast(F32)
+            for first in range(0, n_tiles, PAIR):
+                turned = psum_ring.tile([P, 2, PAIR * P], F32, tag="bank")
+                for j in range(PAIR):
+                    for u in range(2):
+                        nc.tensor.transpose(
+                            turned[:, u, j * P : (j + 1) * P],
+                            words[:, first + j, u : 2 * P : 2],
+                            ident[:],
+                        )
+                nc.scalar.copy(
+                    out=grouped_words[:, first * P : (first + PAIR) * P, :],
+                    in_=turned[:].rearrange("p u r -> p r u"),
+                )
+            turned_operands.append((grouped, codes, scales))
+            if len(turned_operands) > 1:
+                quantise(turned_operands[-2])
+
+        w_codes = const.tile([P, D], U32, align_bytes=64)
+        w_scales = const.tile([P, D], U8, align_bytes=64)
+        x_codes = const.tile([P, N_BLOCKS, BLOCK], U32, align_bytes=64)
+        x_scales = const.tile([P, N_BLOCKS, BLOCK], U8, align_bytes=64)
+        k_codes = const.tile([P, BATCHES, KEYS], U32, align_bytes=64)
+        k_scales = const.tile([P, BATCHES, KEYS], U8, align_bytes=64)
+
+        transpose_and_quantise(w_raw[:], CHUNKS, w_codes[:], w_scales[:])
+        for b in range(BATCHES):
+            text_raw = raw.tile([P, TILES_PER_BATCH, D], BF16)
+            nc.sync.dma_start(out=text_raw[:], in_=text[b].rearrange("(p i) k -> p i k", i=TILES_PER_BATCH))
+            k_raw = raw.tile([P, KEY_TILES, D], BF16)
+            nc.sync.dma_start(out=k_raw[:], in_=k_norm[b].rearrange("(j p) d -> p j d", p=P))
+            for half in range(BLOCKS_PER_BATCH):
+                n = b * BLOCKS_PER_BATCH + half
+                transpose_and_quantise(
+                    text_raw[:, half * BLOCK_TILES : (half + 1) * BLOCK_TILES, :],
+                    BLOCK_TILES,
+                    x_codes[:, n, :],
+                    x_scales[:, n, :],
+                )
+            transpose_and_quantise(k_raw[:], KEY_TILES, k_codes[:, b, :], k_scales[:, b, :])
+        quantise(turned_operands[-1])
+
+        live = {}
+
+        def project(n):
+            banks = []
+            for c in range(CHUNKS):
+                q_ps = psum_ring.tile([P, BLOCK], F32, tag="bank")
+                nc.tensor.matmul_mx(
+                    out=q_ps[:],
+                    lhsT=w_codes[:, c * P : (c + 1) * P].bitcast(FP8X4),
+                    lhsT_scale=w_scales[:, c * P : (c + 1) * P],
+                    rhs=x_codes[:, n, :].bitcast(FP8X4),
+                    rhs_scale=x_scales[:, n, :],
+                    start=True,
+                    stop=True,
+                )
+                banks.append(q_ps)
+            live["q", n] = banks
+
+        def square(n):
+            squares = stage.tile([P, CHUNKS, BLOCK], F32)
+            halves = deep.tile([P, 2, BLOCK], F32)
+            for c in range(CHUNKS):
+                nc.scalar.activation(
+                    out=squares[:, c, :], in_=live["q", n][c][:], func=ACT.Square, bias=bias[:, c : c + 1], scale=1.0
+                )
+            for h in range(2):
+                nc.gpsimd.tensor_tensor(
+                    out=halves[:, h, :], in0=squares[:, 2 * h, :], in1=squares[:, 2 * h + 1, :], op=ALU.add
+                )
+            live["halves", n] = halves
+
+        def scale_on_vector(n):
+            nc.vector.tensor_scalar(
+                out=live["scaled", n][:, CHUNKS - 1, :],
+                in0=live["q", n][CHUNKS - 1][:],
+                scalar1=gain[:, CHUNKS - 1 : CHUNKS],
+                scalar2=gain_bias[:, CHUNKS - 1 : CHUNKS],
+                op0=ALU.mult,
+                op1=ALU.add,
+            )
+
+        def scale_on_scalar(n):
+            scaled = deeper.tile([P, CHUNKS, BLOCK], F32)
+            live["scaled", n] = scaled
+            for c in range(CHUNKS - 1):
+                nc.scalar.activation(
+                    out=live["scaled", n][:, c, :],
+                    in_=live["q", n][c][:],
+                    func=ACT.Identity,
+                    bias=gain_bias[:, c : c + 1],
+                    scale=gain[:, c : c + 1],
+                )
+
+        def inverse_rms(n):
+            halves = live["halves", n]
+            sums = psum_one.tile([P, BLOCK_TILES], F32)
+            for i in range(BLOCK_TILES):
+                for h in range(2):
+                    nc.tensor.matmul(
+                        out=sums[:, i : i + 1],
+                        lhsT=halves[:, h, i * P : (i + 1) * P],
+                        rhs=ones[:],
+                        start=(h == 0),
+                        stop=(h == 1),
+                    )
+            rstd = deep.tile([P, BLOCK_TILES], F32)
+            nc.scalar.activation(out=rstd[:], in_=sums[:], func=ACT.Abs_reciprocal_sqrt, bias=eps[:], scale=1.0 / D)
+            live["rstd", n] = rstd
+
+        def spread_inverse(n):
+            spread = psum_one.tile([P, BLOCK], F32)
+            for i in range(BLOCK_TILES):
+                nc.tensor.transpose(
+                    spread[:, i * P : (i + 1) * P], live["rstd", n][:, i : i + 1].to_broadcast([P, P]), ident[:]
+                )
+            live["spread", n] = spread
+
+        def normalise(n):
+            q_grouped = stage.tile([P, BLOCK, PACK], BF16, align_bytes=64)
+            nc.vector.tensor_tensor(
+                out=q_grouped[:].rearrange("p (t i) c -> p t c i", i=RUN),
+                in0=live["scaled", n][:].rearrange("p c (t i) -> p t c i", i=RUN),
+                in1=live["spread", n][:]
+                .rearrange("p (t i) -> p t i", i=RUN)
+                .unsqueeze(2)
+                .to_broadcast([P, BLOCK // RUN, PACK, RUN]),
+                op=ALU.mult,
+            )
+            q_codes = deep.tile([P, BLOCK], U32, align_bytes=64)
+            q_scales = deep.tile([P, BLOCK], U8, align_bytes=64)
+            nc.vector.quantize_mx(
+                out=q_codes[:].bitcast(FP8X4), scales=q_scales[:], in_=q_grouped[:].rearrange("p t c -> p (t c)")
+            )
+            live["q_mx", n] = (q_codes, q_scales)
+
+        def score(n):
+            b = n // BLOCKS_PER_BATCH
+            q_codes, q_scales = live["q_mx", n]
+            banks = []
+            for first in range(0, BLOCK_TILES, PAIR):
+                s_ps = psum_ring.tile([P, PAIR, KEYS], F32, tag="bank")
+                for j in range(PAIR):
+                    i = first + j
+                    nc.tensor.matmul_mx(
+                        out=s_ps[:, j, :],
+                        lhsT=q_codes[:, i * P : (i + 1) * P].bitcast(FP8X4),
+                        lhsT_scale=q_scales[:, i * P : (i + 1) * P],
+                        rhs=k_codes[:, b, :].bitcast(FP8X4),
+                        rhs_scale=k_scales[:, b, :],
+                        start=True,
+                        stop=True,
+                    )
+                banks.append(s_ps)
+            live["s", n] = banks
+
+        def store(n):
+            b, half = divmod(n, BLOCKS_PER_BATCH)
+            scores = deep.tile([P, BLOCK_TILES, KEYS], F32)
+            nc.scalar.mul(out=scores[:, 0:PAIR, :], in_=live["s", n][0][:], mul=1.0 / math.sqrt(D))
+            nc.vector.tensor_scalar(
+                out=scores[:, PAIR : 2 * PAIR, :],
+                in0=live["s", n][1][:],
+                scalar1=1.0 / math.sqrt(D),
+                scalar2=None,
+                op0=ALU.mult,
+            )
+            nc.sync.dma_start(
+                out=out[b].rearrange("(p i) s -> p i s", i=TILES_PER_BATCH)[
+                    :, half * BLOCK_TILES : (half + 1) * BLOCK_TILES, :
+                ],
+                in_=scores[:],
+            )
+
+        def run(stage_of_block, n):
+            if 0 <= n < N_BLOCKS:
+                stage_of_block(n)
+
+        for n in range(-2, N_BLOCKS + 2):
+            run(spread_inverse, n)
+            run(scale_on_scalar, n + 1)
+            run(scale_on_vector, n + 1)
+            run(store, n - 2)
+            run(project, n + 2)
+            run(square, n + 2)
+            run(inverse_rms, n + 1)
+            run(score, n - 1)
+            run(normalise, n)

@@ -29,6 +29,7 @@ BLOCKS_PER_BATCH = TOKENS // BLOCK
 N_BLOCKS = BATCHES * BLOCKS_PER_BATCH
 PAIR = 2
 RUN = 4
+LOADS_AHEAD = 8
 
 FLOPS = 2 * BATCHES * TOKENS * D * D + 2 * BATCHES * TOKENS * D * KEYS
 
@@ -38,28 +39,46 @@ def tile_crossattention_pb_t_kernel(tc, text, Wq_w, Wq_b, qn_w, k_norm, out):
     with ExitStack() as ctx:
         ctx.enter_context(tc.manual_schedule())
         const = ctx.enter_context(tc.tile_pool(name="const", bufs=1))
-        raw = ctx.enter_context(tc.tile_pool(name="raw", bufs=4))
+        raw = ctx.enter_context(tc.tile_pool(name="raw", bufs=LOADS_AHEAD))
+        raw_keys = ctx.enter_context(tc.tile_pool(name="raw_keys", bufs=LOADS_AHEAD // BLOCKS_PER_BATCH))
         stage = ctx.enter_context(tc.tile_pool(name="stage", bufs=2))
         deep = ctx.enter_context(tc.tile_pool(name="deep", bufs=3))
         deeper = ctx.enter_context(tc.tile_pool(name="deeper", bufs=4))
+        ahead = ctx.enter_context(tc.tile_pool(name="ahead", bufs=N_BLOCKS))
+
         psum_ring = ctx.enter_context(tc.psum_pool(name="psum_ring", bufs=6))
         psum_one = ctx.enter_context(tc.psum_pool(name="psum_one", bufs=1))
 
         w_raw = const.tile([P, CHUNKS, D], BF16)
-        nc.sync.dma_start(
-            out=w_raw[:],
-            in_=Wq_w.rearrange("(p c) k -> p c k", c=CHUNKS),
-        )
+        for first in range(0, CHUNKS, PAIR):
+            nc.sync.dma_start(
+                out=w_raw[:, first : first + PAIR, :],
+                in_=Wq_w.rearrange("(p c) k -> p c k", c=CHUNKS)[:, first : first + PAIR, :],
+            )
         bias_bf = const.tile([P, CHUNKS], BF16)
         gain_bf = const.tile([P, CHUNKS], BF16)
-        nc.scalar.dma_start(
-            out=bias_bf[:],
-            in_=Wq_b.rearrange("(p c) -> p c", c=CHUNKS),
-        )
-        nc.scalar.dma_start(
-            out=gain_bf[:],
-            in_=qn_w.rearrange("(p c) -> p c", c=CHUNKS),
-        )
+        nc.scalar.dma_start(out=bias_bf[:], in_=Wq_b.rearrange("(p c) -> p c", c=CHUNKS))
+        nc.scalar.dma_start(out=gain_bf[:], in_=qn_w.rearrange("(p c) -> p c", c=CHUNKS))
+        live = {}
+
+        def load(n):
+            b, half = divmod(n, BLOCKS_PER_BATCH)
+            text_raw = raw.tile([P, BLOCK_TILES, D], BF16)
+            nc.sync.dma_start(
+                out=text_raw[:],
+                in_=text[b].rearrange("(p i) k -> p i k", i=TILES_PER_BATCH)[
+                    :, half * BLOCK_TILES : (half + 1) * BLOCK_TILES, :
+                ],
+            )
+            live["text_raw", n] = text_raw
+            if half == 0:
+                k_raw = raw_keys.tile([P, KEY_TILES, D], BF16)
+                nc.sync.dma_start(out=k_raw[:], in_=k_norm[b].rearrange("(j p) d -> p j d", p=P))
+                live["k_raw", n] = k_raw
+
+        for n in range(LOADS_AHEAD):
+            load(n)
+
         ident = const.tile([P, P], F32)
         make_identity(nc, ident[:])
         ones = const.tile([P, 1], F32)
@@ -69,139 +88,147 @@ def tile_crossattention_pb_t_kernel(tc, text, Wq_w, Wq_b, qn_w, k_norm, out):
         bias = const.tile([P, CHUNKS], F32)
         gain = const.tile([P, CHUNKS], F32)
         gain_bias = const.tile([P, CHUNKS], F32)
-        nc.vector.tensor_copy(out=bias[:], in_=bias_bf[:])
-        nc.vector.tensor_copy(out=gain[:], in_=gain_bf[:])
-        nc.vector.tensor_tensor(out=gain_bias[:], in0=gain[:], in1=bias[:], op=ALU.mult)
 
-        turned_operands = []
+        w_codes = const.tile([P, D], U32, align_bytes=64)
+        w_scales = const.tile([P, D], U8, align_bytes=64)
+        k_codes = const.tile([P, BATCHES, KEYS], U32, align_bytes=64)
+        k_scales = const.tile([P, BATCHES, KEYS], U8, align_bytes=64)
 
-        def quantise(operand):
-            grouped, codes, scales = operand
-            nc.vector.quantize_mx(
-                out=codes.bitcast(FP8X4),
-                scales=scales,
-                in_=grouped[:].rearrange("p r t -> p (r t)"),
-            )
-
-        def transpose_and_quantise(rows, n_tiles, codes, scales):
+        def turn(rows, n_tiles, copies):
             words = rows.bitcast(F32)
             grouped = deep.tile([P, n_tiles * P, PACK], BF16, align_bytes=64, tag="grouped%d" % n_tiles)
             grouped_words = grouped[:].bitcast(F32)
-            for first in range(0, n_tiles, PAIR):
+            for copy, first in zip(copies, range(0, n_tiles, PAIR)):
                 turned = psum_ring.tile([P, 2, PAIR * P], F32, tag="bank")
                 for j in range(PAIR):
                     for u in range(2):
                         nc.tensor.transpose(
-                            turned[:, u, j * P : (j + 1) * P],
-                            words[:, first + j, u : 2 * P : 2],
-                            ident[:],
+                            turned[:, u, j * P : (j + 1) * P], words[:, first + j, u : 2 * P : 2], ident[:]
                         )
-                nc.scalar.copy(
+                copy(
                     out=grouped_words[:, first * P : (first + PAIR) * P, :],
                     in_=turned[:].rearrange("p u r -> p r u"),
                 )
-            turned_operands.append((grouped, codes, scales))
-            if len(turned_operands) > 1:
-                quantise(turned_operands[-2])
+            return grouped
 
-        w_codes = const.tile([P, D], U32, align_bytes=64)
-        w_scales = const.tile([P, D], U8, align_bytes=64)
-        x_codes = const.tile([P, N_BLOCKS, BLOCK], U32, align_bytes=64)
-        x_scales = const.tile([P, N_BLOCKS, BLOCK], U8, align_bytes=64)
-        k_codes = const.tile([P, BATCHES, KEYS], U32, align_bytes=64)
-        k_scales = const.tile([P, BATCHES, KEYS], U8, align_bytes=64)
+        def quantise(grouped, codes, scales):
+            nc.vector.quantize_mx(
+                out=codes.bitcast(FP8X4), scales=scales, in_=grouped[:].rearrange("p r t -> p (r t)")
+            )
 
-        transpose_and_quantise(w_raw[:], CHUNKS, w_codes[:], w_scales[:])
-        for b in range(BATCHES):
-            text_raw = raw.tile([P, TILES_PER_BATCH, D], BF16)
-            nc.sync.dma_start(out=text_raw[:], in_=text[b].rearrange("(p i) k -> p i k", i=TILES_PER_BATCH))
-            k_raw = raw.tile([P, KEY_TILES, D], BF16)
-            nc.sync.dma_start(out=k_raw[:], in_=k_norm[b].rearrange("(j p) d -> p j d", p=P))
-            for half in range(BLOCKS_PER_BATCH):
-                n = b * BLOCKS_PER_BATCH + half
-                transpose_and_quantise(
-                    text_raw[:, half * BLOCK_TILES : (half + 1) * BLOCK_TILES, :],
-                    BLOCK_TILES,
-                    x_codes[:, n, :],
-                    x_scales[:, n, :],
-                )
-            transpose_and_quantise(k_raw[:], KEY_TILES, k_codes[:, b, :], k_scales[:, b, :])
-        quantise(turned_operands[-1])
+        w_grouped = turn(w_raw[:], CHUNKS, [nc.scalar.copy, nc.vector.tensor_copy])
 
-        live = {}
+        def turn_text(n):
+            copies = [nc.scalar.copy, nc.vector.tensor_copy]
+            live["text", n] = turn(live["text_raw", n][:], BLOCK_TILES, copies)
 
-        def project(n):
-            banks = []
-            for c in range(CHUNKS):
+        def turn_keys(n):
+            if n % BLOCKS_PER_BATCH == 0:
+                live["keys", n] = turn(live["k_raw", n][:], KEY_TILES, [nc.scalar.copy])
+
+        def quantise_text(n):
+            x_codes = ahead.tile([P, BLOCK], U32, align_bytes=64)
+            x_scales = ahead.tile([P, BLOCK], U8, align_bytes=64)
+            quantise(live["text", n], x_codes[:], x_scales[:])
+            live["x_mx", n] = (x_codes, x_scales)
+
+        def quantise_keys(n):
+            if n % BLOCKS_PER_BATCH == 0:
+                b = n // BLOCKS_PER_BATCH
+                quantise(live["keys", n], k_codes[:, b, :], k_scales[:, b, :])
+
+        def project(n, chunks):
+            x_codes, x_scales = live["x_mx", n]
+            banks = live.setdefault(("q", n), [])
+            for c in chunks:
                 q_ps = psum_ring.tile([P, BLOCK], F32, tag="bank")
                 nc.tensor.matmul_mx(
                     out=q_ps[:],
                     lhsT=w_codes[:, c * P : (c + 1) * P].bitcast(FP8X4),
                     lhsT_scale=w_scales[:, c * P : (c + 1) * P],
-                    rhs=x_codes[:, n, :].bitcast(FP8X4),
-                    rhs_scale=x_scales[:, n, :],
+                    rhs=x_codes[:].bitcast(FP8X4),
+                    rhs_scale=x_scales[:],
                     start=True,
                     stop=True,
                 )
                 banks.append(q_ps)
-            live["q", n] = banks
 
-        def square(n):
-            squares = stage.tile([P, CHUNKS, BLOCK], F32)
-            halves = deep.tile([P, 2, BLOCK], F32)
-            for c in range(CHUNKS):
+        def square(n, chunks=tuple(range(CHUNKS))):
+            if 0 in chunks:
+                squares = stage.tile([P, CHUNKS, BLOCK], F32)
+                live["squares", n] = squares
+            for c in chunks:
                 nc.scalar.activation(
-                    out=squares[:, c, :], in_=live["q", n][c][:], func=ACT.Square, bias=bias[:, c : c + 1], scale=1.0
+                    out=live["squares", n][:, c, :],
+                    in_=live["q", n][c][:],
+                    func=ACT.Square,
+                    bias=bias[:, c : c + 1],
+                    scale=1.0,
                 )
+
+        def add_up(n):
+            squares = live["squares", n]
+            halves = stage.tile([P, 2, BLOCK], F32)
+            total = deep.tile([P, BLOCK], F32)
             for h in range(2):
                 nc.gpsimd.tensor_tensor(
                     out=halves[:, h, :], in0=squares[:, 2 * h, :], in1=squares[:, 2 * h + 1, :], op=ALU.add
                 )
-            live["halves", n] = halves
+            nc.gpsimd.tensor_tensor(out=total[:], in0=halves[:, 0, :], in1=halves[:, 1, :], op=ALU.add)
+            live["total", n] = total
 
-        def scale_on_vector(n):
-            nc.vector.tensor_scalar(
-                out=live["scaled", n][:, CHUNKS - 1, :],
-                in0=live["q", n][CHUNKS - 1][:],
-                scalar1=gain[:, CHUNKS - 1 : CHUNKS],
-                scalar2=gain_bias[:, CHUNKS - 1 : CHUNKS],
-                op0=ALU.mult,
-                op1=ALU.add,
-            )
+        def scaled_tile(n):
+            if ("scaled", n) not in live:
+                scaled = deeper.tile([P, CHUNKS, BLOCK], F32)
+                live["scaled", n] = scaled
+            return live["scaled", n]
 
-        def scale_on_scalar(n):
-            scaled = deeper.tile([P, CHUNKS, BLOCK], F32)
-            live["scaled", n] = scaled
-            for c in range(CHUNKS - 1):
+        def scale_on_vector(n, chunks):
+            for c in chunks:
+                nc.vector.tensor_scalar(
+                    out=scaled_tile(n)[:, c, :],
+                    in0=live["q", n][c][:],
+                    scalar1=gain[:, c : c + 1],
+                    scalar2=gain_bias[:, c : c + 1],
+                    op0=ALU.mult,
+                    op1=ALU.add,
+                )
+
+        def scale_on_scalar(n, chunks):
+            for c in chunks:
                 nc.scalar.activation(
-                    out=live["scaled", n][:, c, :],
+                    out=scaled_tile(n)[:, c, :],
                     in_=live["q", n][c][:],
                     func=ACT.Identity,
                     bias=gain_bias[:, c : c + 1],
                     scale=gain[:, c : c + 1],
                 )
 
-        def inverse_rms(n):
-            halves = live["halves", n]
+        def sum_squares(n):
+            total = live["total", n]
             sums = psum_one.tile([P, BLOCK_TILES], F32)
             for i in range(BLOCK_TILES):
-                for h in range(2):
-                    nc.tensor.matmul(
-                        out=sums[:, i : i + 1],
-                        lhsT=halves[:, h, i * P : (i + 1) * P],
-                        rhs=ones[:],
-                        start=(h == 0),
-                        stop=(h == 1),
-                    )
+                nc.tensor.matmul(
+                    out=sums[:, i : i + 1], lhsT=total[:, i * P : (i + 1) * P], rhs=ones[:], start=True, stop=True
+                )
+            live["sums", n] = sums
+
+        def inverse_rms(n):
             rstd = deep.tile([P, BLOCK_TILES], F32)
-            nc.scalar.activation(out=rstd[:], in_=sums[:], func=ACT.Abs_reciprocal_sqrt, bias=eps[:], scale=1.0 / D)
+            nc.scalar.activation(
+                out=rstd[:], in_=live["sums", n][:], func=ACT.Abs_reciprocal_sqrt, bias=eps[:], scale=1.0 / D
+            )
             live["rstd", n] = rstd
 
         def spread_inverse(n):
             spread = psum_one.tile([P, BLOCK], F32)
             for i in range(BLOCK_TILES):
-                nc.tensor.transpose(
-                    spread[:, i * P : (i + 1) * P], live["rstd", n][:, i : i + 1].to_broadcast([P, P]), ident[:]
+                nc.tensor.matmul(
+                    out=spread[:, i * P : (i + 1) * P],
+                    lhsT=live["rstd", n][:, i : i + 1].to_broadcast([P, P]),
+                    rhs=ident[:],
+                    start=True,
+                    stop=True,
                 )
             live["spread", n] = spread
 
@@ -216,11 +243,12 @@ def tile_crossattention_pb_t_kernel(tc, text, Wq_w, Wq_b, qn_w, k_norm, out):
                 .to_broadcast([P, BLOCK // RUN, PACK, RUN]),
                 op=ALU.mult,
             )
+            live["normalised", n] = q_grouped
+
+        def quantise_queries(n):
             q_codes = deep.tile([P, BLOCK], U32, align_bytes=64)
             q_scales = deep.tile([P, BLOCK], U8, align_bytes=64)
-            nc.vector.quantize_mx(
-                out=q_codes[:].bitcast(FP8X4), scales=q_scales[:], in_=q_grouped[:].rearrange("p t c -> p (t c)")
-            )
+            quantise(live["normalised", n], q_codes[:], q_scales[:])
             live["q_mx", n] = (q_codes, q_scales)
 
         def score(n):
@@ -243,35 +271,68 @@ def tile_crossattention_pb_t_kernel(tc, text, Wq_w, Wq_b, qn_w, k_norm, out):
                 banks.append(s_ps)
             live["s", n] = banks
 
+        def drain_on_vector(n, banks):
+            for j in banks:
+                nc.vector.tensor_scalar(
+                    out=scores_tile(n)[:, j * PAIR : (j + 1) * PAIR, :],
+                    in0=live["s", n][j][:],
+                    scalar1=1.0 / math.sqrt(D),
+                    scalar2=None,
+                    op0=ALU.mult,
+                )
+
+        def drain_on_scalar(n, banks):
+            for j in banks:
+                nc.scalar.mul(
+                    out=scores_tile(n)[:, j * PAIR : (j + 1) * PAIR, :], in_=live["s", n][j][:], mul=1.0 / math.sqrt(D)
+                )
+
+        def scores_tile(n):
+            if ("scores", n) not in live:
+                scores = deep.tile([P, BLOCK_TILES, KEYS], F32)
+                live["scores", n] = scores
+            return live["scores", n]
+
         def store(n):
             b, half = divmod(n, BLOCKS_PER_BATCH)
-            scores = deep.tile([P, BLOCK_TILES, KEYS], F32)
-            nc.scalar.mul(out=scores[:, 0:PAIR, :], in_=live["s", n][0][:], mul=1.0 / math.sqrt(D))
-            nc.vector.tensor_scalar(
-                out=scores[:, PAIR : 2 * PAIR, :],
-                in0=live["s", n][1][:],
-                scalar1=1.0 / math.sqrt(D),
-                scalar2=None,
-                op0=ALU.mult,
-            )
             nc.sync.dma_start(
                 out=out[b].rearrange("(p i) s -> p i s", i=TILES_PER_BATCH)[
                     :, half * BLOCK_TILES : (half + 1) * BLOCK_TILES, :
                 ],
-                in_=scores[:],
+                in_=live["scores", n][:],
             )
 
-        def run(stage_of_block, n):
+        def run(stage_of_block, n, *more):
             if 0 <= n < N_BLOCKS:
-                stage_of_block(n)
+                stage_of_block(n, *more)
+
+        for n in range(N_BLOCKS):
+            turn_text(n)
+            turn_keys(n)
+            if n + LOADS_AHEAD < N_BLOCKS:
+                load(n + LOADS_AHEAD)
+            if n == 0:
+                quantise(w_grouped, w_codes[:], w_scales[:])
+                nc.vector.tensor_copy(out=bias[:], in_=bias_bf[:])
+                nc.vector.tensor_copy(out=gain[:], in_=gain_bf[:])
+                nc.vector.tensor_tensor(out=gain_bias[:], in0=gain[:], in1=bias[:], op=ALU.mult)
+            else:
+                quantise_text(n - 1)
+                quantise_keys(n - 1)
+        quantise_text(N_BLOCKS - 1)
 
         for n in range(-2, N_BLOCKS + 2):
-            run(spread_inverse, n)
-            run(scale_on_scalar, n + 1)
-            run(scale_on_vector, n + 1)
+            run(sum_squares, n)
+            run(scale_on_scalar, n + 1, (0, 1, 2))
+            run(scale_on_vector, n + 1, (3,))
+            run(inverse_rms, n)
+            run(drain_on_scalar, n - 2, (0,))
+            run(drain_on_vector, n - 2, (1,))
             run(store, n - 2)
-            run(project, n + 2)
+            run(quantise_queries, n - 1)
+            run(project, n + 2, (0, 1, 2, 3))
+            run(spread_inverse, n)
             run(square, n + 2)
-            run(inverse_rms, n + 1)
+            run(add_up, n + 2)
             run(score, n - 1)
             run(normalise, n)

@@ -11,6 +11,7 @@ U8 = mybir.dt.uint8
 FP8X4 = mybir.dt.float8_e4m3fn_x4
 ACT = mybir.ActivationFunctionType
 ALU = mybir.AluOpType
+AX = mybir.AxisListType
 
 P = 128
 PACK = 4
@@ -81,10 +82,10 @@ def tile_crossattention_pb_t_kernel(tc, text, Wq_w, Wq_b, qn_w, k_norm, out):
 
         ident = const.tile([P, P], F32)
         make_identity(nc, ident[:])
-        ones = const.tile([P, 1], F32)
-        nc.vector.memset(ones[:], 1.0)
         eps = const.tile([P, 1], F32)
         nc.vector.memset(eps[:], EPS)
+        table = const.tile([P, 1], F32)
+        nc.scalar.activation(out=table[:], in_=eps[:], func=ACT.Abs_reciprocal_sqrt, bias=eps[:], scale=1.0)
         bias = const.tile([P, CHUNKS], F32)
         gain = const.tile([P, CHUNKS], F32)
         gain_bias = const.tile([P, CHUNKS], F32)
@@ -166,17 +167,6 @@ def tile_crossattention_pb_t_kernel(tc, text, Wq_w, Wq_b, qn_w, k_norm, out):
                     scale=1.0,
                 )
 
-        def add_up(n):
-            squares = live["squares", n]
-            halves = stage.tile([P, 2, BLOCK], F32)
-            total = deep.tile([P, BLOCK], F32)
-            for h in range(2):
-                nc.gpsimd.tensor_tensor(
-                    out=halves[:, h, :], in0=squares[:, 2 * h, :], in1=squares[:, 2 * h + 1, :], op=ALU.add
-                )
-            nc.gpsimd.tensor_tensor(out=total[:], in0=halves[:, 0, :], in1=halves[:, 1, :], op=ALU.add)
-            live["total", n] = total
-
         def scaled_tile(n):
             if ("scaled", n) not in live:
                 scaled = deeper.tile([P, CHUNKS, BLOCK], F32)
@@ -204,13 +194,24 @@ def tile_crossattention_pb_t_kernel(tc, text, Wq_w, Wq_b, qn_w, k_norm, out):
                     scale=gain[:, c : c + 1],
                 )
 
-        def sum_squares(n):
-            total = live["total", n]
-            sums = psum_one.tile([P, BLOCK_TILES], F32)
+        def turn_squares(n):
+            squares = live["squares", n]
+            turned_sq = psum_one.tile([P, BLOCK_TILES, P], F32)
             for i in range(BLOCK_TILES):
-                nc.tensor.matmul(
-                    out=sums[:, i : i + 1], lhsT=total[:, i * P : (i + 1) * P], rhs=ones[:], start=True, stop=True
-                )
+                for c in range(CHUNKS):
+                    nc.tensor.matmul(
+                        out=turned_sq[:, i, :],
+                        lhsT=squares[:, c, i * P : (i + 1) * P],
+                        rhs=ident[:],
+                        start=(c == 0),
+                        stop=(c == CHUNKS - 1),
+                        is_transpose=True,
+                    )
+            live["turned_sq", n] = turned_sq
+
+        def sum_squares(n):
+            sums = deep.tile([P, BLOCK_TILES], F32)
+            nc.vector.tensor_reduce(out=sums[:], in_=live["turned_sq", n][:], axis=AX.X, op=ALU.add)
             live["sums", n] = sums
 
         def inverse_rms(n):
@@ -223,59 +224,66 @@ def tile_crossattention_pb_t_kernel(tc, text, Wq_w, Wq_b, qn_w, k_norm, out):
         def spread_inverse(n):
             spread = psum_one.tile([P, BLOCK], F32)
             for i in range(BLOCK_TILES):
-                nc.tensor.matmul(
-                    out=spread[:, i * P : (i + 1) * P],
-                    lhsT=live["rstd", n][:, i : i + 1].to_broadcast([P, P]),
-                    rhs=ident[:],
-                    start=True,
-                    stop=True,
+                nc.tensor.transpose(
+                    spread[:, i * P : (i + 1) * P], live["rstd", n][:, i : i + 1].to_broadcast([P, P]), ident[:]
                 )
             live["spread", n] = spread
 
-        def normalise(n):
-            q_grouped = stage.tile([P, BLOCK, PACK], BF16, align_bytes=64)
-            nc.vector.tensor_tensor(
-                out=q_grouped[:].rearrange("p (t i) c -> p t c i", i=RUN),
-                in0=live["scaled", n][:].rearrange("p c (t i) -> p t c i", i=RUN),
-                in1=live["spread", n][:]
-                .rearrange("p (t i) -> p t i", i=RUN)
-                .unsqueeze(2)
-                .to_broadcast([P, BLOCK // RUN, PACK, RUN]),
-                op=ALU.mult,
-            )
-            live["normalised", n] = q_grouped
+        def copy_spread(n, pair):
+            spread_copy = stage.tile([P, PAIR * P], F32)
+            nc.scalar.copy(out=spread_copy[:], in_=live["spread", n][:, pair * PAIR * P : (pair + 1) * PAIR * P])
+            live["spread_copy", n, pair] = spread_copy
 
-        def quantise_queries(n):
-            q_codes = deep.tile([P, BLOCK], U32, align_bytes=64)
-            q_scales = deep.tile([P, BLOCK], U8, align_bytes=64)
-            quantise(live["normalised", n], q_codes[:], q_scales[:])
-            live["q_mx", n] = (q_codes, q_scales)
+        def normalise(engine, n, pair, spread, pieces):
+            q_grouped = deep.tile([P, PAIR * P, PACK], BF16, align_bytes=64)
+            tokens = PAIR * P // pieces
+            for piece in range(pieces):
+                part = slice(piece * tokens, (piece + 1) * tokens)
+                first = pair * PAIR * P + piece * tokens
+                engine.tensor_tensor(
+                    out=q_grouped[:, part, :].rearrange("p (t i) c -> p t c i", i=RUN),
+                    in0=live["scaled", n][:, :, first : first + tokens].rearrange("p c (t i) -> p t c i", i=RUN),
+                    in1=spread[:, part]
+                    .rearrange("p (t i) -> p t i", i=RUN)
+                    .unsqueeze(2)
+                    .to_broadcast([P, tokens // RUN, PACK, RUN]),
+                    op=ALU.mult,
+                )
+            live["normalised", n, pair] = q_grouped
 
-        def score(n):
+        def normalise_on_vector(n, pair):
+            normalise(nc.vector, n, pair, live["spread", n][:, pair * PAIR * P : (pair + 1) * PAIR * P], 1)
+
+        def normalise_on_gpsimd(n, pair):
+            normalise(nc.gpsimd, n, pair, live["spread_copy", n, pair][:], 2)
+
+        def quantise_queries(n, pair):
+            q_codes = deep.tile([P, PAIR * P], U32, align_bytes=64)
+            q_scales = deep.tile([P, PAIR * P], U8, align_bytes=64)
+            quantise(live["normalised", n, pair], q_codes[:], q_scales[:])
+            live["q_mx", n, pair] = (q_codes, q_scales)
+
+        def score(n, pair):
             b = n // BLOCKS_PER_BATCH
-            q_codes, q_scales = live["q_mx", n]
-            banks = []
-            for first in range(0, BLOCK_TILES, PAIR):
-                s_ps = psum_ring.tile([P, PAIR, KEYS], F32, tag="bank")
-                for j in range(PAIR):
-                    i = first + j
-                    nc.tensor.matmul_mx(
-                        out=s_ps[:, j, :],
-                        lhsT=q_codes[:, i * P : (i + 1) * P].bitcast(FP8X4),
-                        lhsT_scale=q_scales[:, i * P : (i + 1) * P],
-                        rhs=k_codes[:, b, :].bitcast(FP8X4),
-                        rhs_scale=k_scales[:, b, :],
-                        start=True,
-                        stop=True,
-                    )
-                banks.append(s_ps)
-            live["s", n] = banks
+            q_codes, q_scales = live["q_mx", n, pair]
+            s_ps = psum_ring.tile([P, PAIR, KEYS], F32, tag="bank")
+            for j in range(PAIR):
+                nc.tensor.matmul_mx(
+                    out=s_ps[:, j, :],
+                    lhsT=q_codes[:, j * P : (j + 1) * P].bitcast(FP8X4),
+                    lhsT_scale=q_scales[:, j * P : (j + 1) * P],
+                    rhs=k_codes[:, b, :].bitcast(FP8X4),
+                    rhs_scale=k_scales[:, b, :],
+                    start=True,
+                    stop=True,
+                )
+            live["s", n, pair] = s_ps
 
         def drain_on_vector(n, banks):
             for j in banks:
                 nc.vector.tensor_scalar(
                     out=scores_tile(n)[:, j * PAIR : (j + 1) * PAIR, :],
-                    in0=live["s", n][j][:],
+                    in0=live["s", n, j][:],
                     scalar1=1.0 / math.sqrt(D),
                     scalar2=None,
                     op0=ALU.mult,
@@ -284,7 +292,7 @@ def tile_crossattention_pb_t_kernel(tc, text, Wq_w, Wq_b, qn_w, k_norm, out):
         def drain_on_scalar(n, banks):
             for j in banks:
                 nc.scalar.mul(
-                    out=scores_tile(n)[:, j * PAIR : (j + 1) * PAIR, :], in_=live["s", n][j][:], mul=1.0 / math.sqrt(D)
+                    out=scores_tile(n)[:, j * PAIR : (j + 1) * PAIR, :], in_=live["s", n, j][:], mul=1.0 / math.sqrt(D)
                 )
 
         def scores_tile(n):
@@ -321,18 +329,25 @@ def tile_crossattention_pb_t_kernel(tc, text, Wq_w, Wq_b, qn_w, k_norm, out):
                 quantise_keys(n - 1)
         quantise_text(N_BLOCKS - 1)
 
-        for n in range(-2, N_BLOCKS + 2):
-            run(sum_squares, n)
-            run(scale_on_scalar, n + 1, (0, 1, 2))
-            run(scale_on_vector, n + 1, (3,))
-            run(inverse_rms, n)
-            run(drain_on_scalar, n - 2, (0,))
-            run(drain_on_vector, n - 2, (1,))
+        for n in range(-1, N_BLOCKS + 2):
+            run(square, n, (0, 1))
+            run(project, n, (2, 3))
+            run(quantise_queries, n - 2, 0)
+            run(sum_squares, n - 1)
+            run(scale_on_scalar, n, (0,))
+            run(score, n - 2, 0)
+            run(inverse_rms, n - 1)
+            run(scale_on_scalar, n, (1,))
+            run(scale_on_vector, n, (3,))
+            run(quantise_queries, n - 2, 1)
+            run(spread_inverse, n - 1)
+            run(project, n + 1, (0, 1))
+            run(score, n - 2, 1)
+            run(normalise_on_vector, n - 1, 0)
+            run(square, n, (2, 3))
+            run(copy_spread, n - 1, 1)
+            run(turn_squares, n)
+            run(scale_on_scalar, n, (2,))
+            run(normalise_on_gpsimd, n - 1, 1)
+            run(drain_on_vector, n - 2, (0, 1))
             run(store, n - 2)
-            run(quantise_queries, n - 1)
-            run(project, n + 2, (0, 1, 2, 3))
-            run(spread_inverse, n)
-            run(square, n + 2)
-            run(add_up, n + 2)
-            run(score, n - 1)
-            run(normalise, n)

@@ -338,16 +338,16 @@ def tile_crossattention_pb_t_kernel(tc, text, Wq_w, Wq_b, qn_w, k_norm, out):
             run(score, n - 2, 0)
             run(inverse_rms, n - 1)
             run(scale_on_scalar, n, (1,))
-            run(scale_on_vector, n, (3,))
             run(quantise_queries, n - 2, 1)
+            run(scale_on_vector, n, (3,))
             run(spread_inverse, n - 1)
+            run(drain_on_vector, n - 2, (0,))
             run(project, n + 1, (0, 1))
             run(score, n - 2, 1)
             run(normalise_on_vector, n - 1, 0)
             run(square, n, (2, 3))
-            run(copy_spread, n - 1, 1)
             run(turn_squares, n)
             run(scale_on_scalar, n, (2,))
-            run(normalise_on_gpsimd, n - 1, 1)
-            run(drain_on_vector, n - 2, (0, 1))
+            run(normalise_on_vector, n - 1, 1)
+            run(drain_on_scalar, n - 2, (1,))
             run(store, n - 2)

@@ -30,6 +30,9 @@ BLOCKS_PER_BATCH = TOKENS // BLOCK
 N_BLOCKS = BATCHES * BLOCKS_PER_BATCH
 PAIR = 2
 RUN = 4
+Q_BANKS = ["q0", "q1", "q2", "q3"]
+SCORE_BANKS = ["s0", "s1"]
+FIRST = 15
 LOADS_AHEAD = 8
 
 FLOPS = 2 * BATCHES * TOKENS * D * D + 2 * BATCHES * TOKENS * D * KEYS
@@ -47,8 +50,7 @@ def tile_crossattention_pb_t_kernel(tc, text, Wq_w, Wq_b, qn_w, k_norm, out):
         deeper = ctx.enter_context(tc.tile_pool(name="deeper", bufs=4))
         ahead = ctx.enter_context(tc.tile_pool(name="ahead", bufs=N_BLOCKS))
 
-        psum_ring = ctx.enter_context(tc.psum_pool(name="psum_ring", bufs=6))
-        psum_one = ctx.enter_context(tc.psum_pool(name="psum_one", bufs=1))
+        psum = ctx.enter_context(tc.psum_pool(name="psum", bufs=1))
 
         w_raw = const.tile([P, CHUNKS, D], BF16)
         for first in range(0, CHUNKS, PAIR):
@@ -95,12 +97,12 @@ def tile_crossattention_pb_t_kernel(tc, text, Wq_w, Wq_b, qn_w, k_norm, out):
         k_codes = const.tile([P, BATCHES, KEYS], U32, align_bytes=64)
         k_scales = const.tile([P, BATCHES, KEYS], U8, align_bytes=64)
 
-        def turn(rows, n_tiles, copies):
+        def turn(rows, n_tiles, copies, banks):
             words = rows.bitcast(F32)
             grouped = deep.tile([P, n_tiles * P, PACK], BF16, align_bytes=64, tag="grouped%d" % n_tiles)
             grouped_words = grouped[:].bitcast(F32)
-            for copy, first in zip(copies, range(0, n_tiles, PAIR)):
-                turned = psum_ring.tile([P, 2, PAIR * P], F32, tag="bank")
+            for copy, bank, first in zip(copies, banks, range(0, n_tiles, PAIR)):
+                turned = psum.tile([P, 2, PAIR * P], F32, tag=bank)
                 for j in range(PAIR):
                     for u in range(2):
                         nc.tensor.transpose(
@@ -112,20 +114,28 @@ def tile_crossattention_pb_t_kernel(tc, text, Wq_w, Wq_b, qn_w, k_norm, out):
                 )
             return grouped
 
+        turned_so_far = []
+
+        def next_banks(count):
+            banks = [(Q_BANKS + SCORE_BANKS)[(len(turned_so_far) + i) % 6] for i in range(count)]
+            turned_so_far.extend(banks)
+            return banks
+
         def quantise(grouped, codes, scales):
             nc.vector.quantize_mx(
                 out=codes.bitcast(FP8X4), scales=scales, in_=grouped[:].rearrange("p r t -> p (r t)")
             )
 
-        w_grouped = turn(w_raw[:], CHUNKS, [nc.scalar.copy, nc.vector.tensor_copy])
+        w_grouped = turn(w_raw[:], CHUNKS, [nc.scalar.copy, nc.vector.tensor_copy], next_banks(2))
 
         def turn_text(n):
-            copies = [nc.scalar.copy, nc.vector.tensor_copy]
-            live["text", n] = turn(live["text_raw", n][:], BLOCK_TILES, copies)
+            copies = [nc.scalar.copy if n < FIRST else nc.vector.tensor_copy, nc.vector.tensor_copy]
+            banks = next_banks(2) if n < FIRST else SCORE_BANKS
+            live["text", n] = turn(live["text_raw", n][:], BLOCK_TILES, copies, banks)
 
         def turn_keys(n):
             if n % BLOCKS_PER_BATCH == 0:
-                live["keys", n] = turn(live["k_raw", n][:], KEY_TILES, [nc.scalar.copy])
+                live["keys", n] = turn(live["k_raw", n][:], KEY_TILES, [nc.scalar.copy], next_banks(1))
 
         def quantise_text(n):
             x_codes = ahead.tile([P, BLOCK], U32, align_bytes=64)
@@ -142,7 +152,7 @@ def tile_crossattention_pb_t_kernel(tc, text, Wq_w, Wq_b, qn_w, k_norm, out):
             x_codes, x_scales = live["x_mx", n]
             banks = live.setdefault(("q", n), [])
             for c in chunks:
-                q_ps = psum_ring.tile([P, BLOCK], F32, tag="bank")
+                q_ps = psum.tile([P, BLOCK], F32, tag=Q_BANKS[c])
                 nc.tensor.matmul_mx(
                     out=q_ps[:],
                     lhsT=w_codes[:, c * P : (c + 1) * P].bitcast(FP8X4),
@@ -196,7 +206,7 @@ def tile_crossattention_pb_t_kernel(tc, text, Wq_w, Wq_b, qn_w, k_norm, out):
 
         def turn_squares(n):
             squares = live["squares", n]
-            turned_sq = psum_one.tile([P, BLOCK_TILES, P], F32)
+            turned_sq = psum.tile([P, BLOCK_TILES, P], F32)
             for i in range(BLOCK_TILES):
                 for c in range(CHUNKS):
                     nc.tensor.matmul(
@@ -222,40 +232,41 @@ def tile_crossattention_pb_t_kernel(tc, text, Wq_w, Wq_b, qn_w, k_norm, out):
             live["rstd", n] = rstd
 
         def spread_inverse(n):
-            spread = psum_one.tile([P, BLOCK], F32)
+            spread = psum.tile([P, BLOCK], F32)
             for i in range(BLOCK_TILES):
                 nc.tensor.transpose(
                     spread[:, i * P : (i + 1) * P], live["rstd", n][:, i : i + 1].to_broadcast([P, P]), ident[:]
                 )
             live["spread", n] = spread
 
-        def copy_spread(n, pair):
-            spread_copy = stage.tile([P, PAIR * P], F32)
-            nc.scalar.copy(out=spread_copy[:], in_=live["spread", n][:, pair * PAIR * P : (pair + 1) * PAIR * P])
-            live["spread_copy", n, pair] = spread_copy
+        def copy_spread(n):
+            spread_copy = stage.tile([P, P], F32)
+            nc.vector.tensor_copy(out=spread_copy[:], in_=live["spread", n][:, BLOCK - P :])
+            live["spread_copy", n] = spread_copy
 
-        def normalise(engine, n, pair, spread, pieces):
-            q_grouped = deep.tile([P, PAIR * P, PACK], BF16, align_bytes=64)
-            tokens = PAIR * P // pieces
-            for piece in range(pieces):
-                part = slice(piece * tokens, (piece + 1) * tokens)
-                first = pair * PAIR * P + piece * tokens
-                engine.tensor_tensor(
-                    out=q_grouped[:, part, :].rearrange("p (t i) c -> p t c i", i=RUN),
-                    in0=live["scaled", n][:, :, first : first + tokens].rearrange("p c (t i) -> p t c i", i=RUN),
-                    in1=spread[:, part]
-                    .rearrange("p (t i) -> p t i", i=RUN)
-                    .unsqueeze(2)
-                    .to_broadcast([P, tokens // RUN, PACK, RUN]),
-                    op=ALU.mult,
-                )
-            live["normalised", n, pair] = q_grouped
+        def normalised_tile(n, pair):
+            if ("normalised", n, pair) not in live:
+                q_grouped = deep.tile([P, PAIR * P, PACK], BF16, align_bytes=64)
+                live["normalised", n, pair] = q_grouped
+            return live["normalised", n, pair]
 
-        def normalise_on_vector(n, pair):
-            normalise(nc.vector, n, pair, live["spread", n][:, pair * PAIR * P : (pair + 1) * PAIR * P], 1)
+        def normalise(engine, n, first, n_tiles, spread):
+            pair, j = divmod(first, PAIR)
+            tokens = n_tiles * P
+            engine.tensor_tensor(
+                out=normalised_tile(n, pair)[:, j * P : j * P + tokens, :].rearrange("p (t i) c -> p t c i", i=RUN),
+                in0=live["scaled", n][:, :, first * P : first * P + tokens].rearrange("p c (t i) -> p t c i", i=RUN),
+                in1=spread.rearrange("p (t i) -> p t i", i=RUN)
+                .unsqueeze(2)
+                .to_broadcast([P, tokens // RUN, PACK, RUN]),
+                op=ALU.mult,
+            )
 
-        def normalise_on_gpsimd(n, pair):
-            normalise(nc.gpsimd, n, pair, live["spread_copy", n, pair][:], 2)
+        def normalise_on_vector(n, first, n_tiles):
+            normalise(nc.vector, n, first, n_tiles, live["spread", n][:, first * P : (first + n_tiles) * P])
+
+        def normalise_on_gpsimd(n):
+            normalise(nc.gpsimd, n, BLOCK_TILES - 1, 1, live["spread_copy", n][:])
 
         def quantise_queries(n, pair):
             q_codes = deep.tile([P, PAIR * P], U32, align_bytes=64)
@@ -266,7 +277,7 @@ def tile_crossattention_pb_t_kernel(tc, text, Wq_w, Wq_b, qn_w, k_norm, out):
         def score(n, pair):
             b = n // BLOCKS_PER_BATCH
             q_codes, q_scales = live["q_mx", n, pair]
-            s_ps = psum_ring.tile([P, PAIR, KEYS], F32, tag="bank")
+            s_ps = psum.tile([P, PAIR, KEYS], F32, tag=SCORE_BANKS[pair])
             for j in range(PAIR):
                 nc.tensor.matmul_mx(
                     out=s_ps[:, j, :],
@@ -301,20 +312,21 @@ def tile_crossattention_pb_t_kernel(tc, text, Wq_w, Wq_b, qn_w, k_norm, out):
                 live["scores", n] = scores
             return live["scores", n]
 
-        def store(n):
+        def store(n, tiles=slice(0, BLOCK_TILES)):
             b, half = divmod(n, BLOCKS_PER_BATCH)
+            first = half * BLOCK_TILES
             nc.sync.dma_start(
                 out=out[b].rearrange("(p i) s -> p i s", i=TILES_PER_BATCH)[
-                    :, half * BLOCK_TILES : (half + 1) * BLOCK_TILES, :
+                    :, first + tiles.start : first + tiles.stop, :
                 ],
-                in_=live["scores", n][:],
+                in_=live["scores", n][:, tiles, :],
             )
 
         def run(stage_of_block, n, *more):
             if 0 <= n < N_BLOCKS:
                 stage_of_block(n, *more)
 
-        for n in range(N_BLOCKS):
+        for n in range(FIRST):
             turn_text(n)
             turn_keys(n)
             if n + LOADS_AHEAD < N_BLOCKS:
@@ -327,27 +339,78 @@ def tile_crossattention_pb_t_kernel(tc, text, Wq_w, Wq_b, qn_w, k_norm, out):
             else:
                 quantise_text(n - 1)
                 quantise_keys(n - 1)
-        quantise_text(N_BLOCKS - 1)
+        quantise_text(FIRST - 1)
+        quantise_keys(FIRST - 1)
 
-        for n in range(-1, N_BLOCKS + 2):
+        for n in range(-1, N_BLOCKS - 1):
             run(square, n, (0, 1))
             run(project, n, (2, 3))
             run(quantise_queries, n - 2, 0)
+            run(quantise_queries, n - 2, 1)
+            run(score, n - 2, 0)
             run(sum_squares, n - 1)
             run(scale_on_scalar, n, (0,))
-            run(score, n - 2, 0)
             run(inverse_rms, n - 1)
             run(scale_on_scalar, n, (1,))
-            run(quantise_queries, n - 2, 1)
             run(scale_on_vector, n, (3,))
             run(spread_inverse, n - 1)
             run(drain_on_vector, n - 2, (0,))
             run(project, n + 1, (0, 1))
             run(score, n - 2, 1)
-            run(normalise_on_vector, n - 1, 0)
+            if FIRST <= n + FIRST < N_BLOCKS:
+                turn_text(n + FIRST)
+                if n + FIRST + LOADS_AHEAD < N_BLOCKS:
+                    load(n + FIRST + LOADS_AHEAD)
+                quantise_text(n + FIRST)
+            run(copy_spread, n - 1)
+            run(normalise_on_gpsimd, n - 1)
+            run(normalise_on_vector, n - 1, 0, 2)
             run(square, n, (2, 3))
             run(turn_squares, n)
             run(scale_on_scalar, n, (2,))
-            run(normalise_on_vector, n - 1, 1)
+            run(normalise_on_vector, n - 1, 2, 1)
             run(drain_on_scalar, n - 2, (1,))
             run(store, n - 2)
+
+        last = N_BLOCKS - 1
+        square(last, (0, 1))
+        project(last, (2, 3))
+        quantise_queries(last - 2, 0)
+        quantise_queries(last - 2, 1)
+        score(last - 2, 0)
+        sum_squares(last - 1)
+        square(last, (2,))
+        inverse_rms(last - 1)
+        square(last, (3,))
+        spread_inverse(last - 1)
+        score(last - 2, 1)
+        drain_on_vector(last - 2, (0,))
+        copy_spread(last - 1)
+        normalise_on_gpsimd(last - 1)
+        turn_squares(last)
+        normalise_on_vector(last - 1, 0, 2)
+        scale_on_scalar(last, (0, 1, 2, 3))
+        drain_on_scalar(last - 2, (1,))
+        store(last - 2)
+        sum_squares(last)
+        normalise_on_vector(last - 1, 2, 1)
+        inverse_rms(last)
+        quantise_queries(last - 1, 0)
+        quantise_queries(last - 1, 1)
+        spread_inverse(last)
+        score(last - 1, 0)
+        score(last - 1, 1)
+        copy_spread(last)
+        normalise_on_gpsimd(last)
+        drain_on_scalar(last - 1, (0, 1))
+        store(last - 1)
+        normalise_on_vector(last, 0, 2)
+        normalise_on_vector(last, 2, 1)
+        quantise_queries(last, 0)
+        quantise_queries(last, 1)
+        score(last, 0)
+        score(last, 1)
+        drain_on_vector(last, (0,))
+        store(last, slice(0, PAIR))
+        drain_on_scalar(last, (1,))
+        store(last, slice(PAIR, BLOCK_TILES))

@@ -33,6 +33,7 @@ RUN = 4
 Q_BANKS = ["q0", "q1", "q2", "q3"]
 SCORE_BANKS = ["s0", "s1"]
 FIRST = 15
+SPLIT = 192
 LOADS_AHEAD = 8
 
 FLOPS = 2 * BATCHES * TOKENS * D * D + 2 * BATCHES * TOKENS * D * KEYS
@@ -177,6 +178,12 @@ def tile_crossattention_pb_t_kernel(tc, text, Wq_w, Wq_b, qn_w, k_norm, out):
                     scale=1.0,
                 )
 
+        def add_pair(n):
+            pair_sum = stage.tile([P, BLOCK], F32)
+            squares = live["squares", n]
+            nc.gpsimd.tensor_tensor(out=pair_sum[:], in0=squares[:, 0, :], in1=squares[:, 1, :], op=ALU.add)
+            live["pair_sum", n] = pair_sum
+
         def scaled_tile(n):
             if ("scaled", n) not in live:
                 scaled = deeper.tile([P, CHUNKS, BLOCK], F32)
@@ -185,20 +192,22 @@ def tile_crossattention_pb_t_kernel(tc, text, Wq_w, Wq_b, qn_w, k_norm, out):
 
         def scale_on_vector(n, chunks):
             for c in chunks:
+                cols = slice(0, SPLIT if c == 2 else BLOCK)
                 nc.vector.tensor_scalar(
-                    out=scaled_tile(n)[:, c, :],
-                    in0=live["q", n][c][:],
+                    out=scaled_tile(n)[:, c, cols],
+                    in0=live["q", n][c][:, cols],
                     scalar1=gain[:, c : c + 1],
                     scalar2=gain_bias[:, c : c + 1],
                     op0=ALU.mult,
                     op1=ALU.add,
                 )
 
-        def scale_on_scalar(n, chunks):
+        def scale_on_scalar(n, chunks, split=SPLIT):
             for c in chunks:
+                cols = slice(split if c == 2 else 0, BLOCK)
                 nc.scalar.activation(
-                    out=scaled_tile(n)[:, c, :],
-                    in_=live["q", n][c][:],
+                    out=scaled_tile(n)[:, c, cols],
+                    in_=live["q", n][c][:, cols],
                     func=ACT.Identity,
                     bias=gain_bias[:, c : c + 1],
                     scale=gain[:, c : c + 1],
@@ -208,13 +217,14 @@ def tile_crossattention_pb_t_kernel(tc, text, Wq_w, Wq_b, qn_w, k_norm, out):
             squares = live["squares", n]
             turned_sq = psum.tile([P, BLOCK_TILES, P], F32)
             for i in range(BLOCK_TILES):
-                for c in range(CHUNKS):
+                parts = [live["pair_sum", n][:], squares[:, 2, :], squares[:, 3, :]]
+                for c, part in enumerate(parts):
                     nc.tensor.matmul(
                         out=turned_sq[:, i, :],
-                        lhsT=squares[:, c, i * P : (i + 1) * P],
+                        lhsT=part[:, i * P : (i + 1) * P],
                         rhs=ident[:],
                         start=(c == 0),
-                        stop=(c == CHUNKS - 1),
+                        stop=(c == len(parts) - 1),
                         is_transpose=True,
                     )
             live["turned_sq", n] = turned_sq
@@ -344,19 +354,20 @@ def tile_crossattention_pb_t_kernel(tc, text, Wq_w, Wq_b, qn_w, k_norm, out):
 
         for n in range(-1, N_BLOCKS - 1):
             run(square, n, (0, 1))
+            run(add_pair, n)
             run(project, n, (2, 3))
             run(quantise_queries, n - 2, 0)
             run(quantise_queries, n - 2, 1)
             run(score, n - 2, 0)
+            run(score, n - 2, 1)
             run(sum_squares, n - 1)
             run(scale_on_scalar, n, (0,))
             run(inverse_rms, n - 1)
             run(scale_on_scalar, n, (1,))
-            run(scale_on_vector, n, (3,))
+            run(scale_on_vector, n, (2, 3))
             run(spread_inverse, n - 1)
             run(drain_on_vector, n - 2, (0,))
             run(project, n + 1, (0, 1))
-            run(score, n - 2, 1)
             if FIRST <= n + FIRST < N_BLOCKS:
                 turn_text(n + FIRST)
                 if n + FIRST + LOADS_AHEAD < N_BLOCKS:
@@ -374,6 +385,7 @@ def tile_crossattention_pb_t_kernel(tc, text, Wq_w, Wq_b, qn_w, k_norm, out):
 
         last = N_BLOCKS - 1
         square(last, (0, 1))
+        add_pair(last)
         project(last, (2, 3))
         quantise_queries(last - 2, 0)
         quantise_queries(last - 2, 1)
@@ -389,12 +401,12 @@ def tile_crossattention_pb_t_kernel(tc, text, Wq_w, Wq_b, qn_w, k_norm, out):
         normalise_on_gpsimd(last - 1)
         turn_squares(last)
         normalise_on_vector(last - 1, 0, 2)
-        scale_on_scalar(last, (0, 1, 2, 3))
-        drain_on_scalar(last - 2, (1,))
-        store(last - 2)
+        scale_on_scalar(last, (0, 1, 2, 3), 0)
         sum_squares(last)
         normalise_on_vector(last - 1, 2, 1)
         inverse_rms(last)
+        drain_on_scalar(last - 2, (1,))
+        store(last - 2)
         quantise_queries(last - 1, 0)
         quantise_queries(last - 1, 1)
         spread_inverse(last)

@@ -34,7 +34,7 @@ Q_BANKS = ["q0", "q1", "q2", "q3"]
 SCORE_BANKS = ["s0", "s1"]
 FIRST = 15
 SPLIT = 192
-LOADS_AHEAD = 8
+LOADS_AHEAD = 4
 
 FLOPS = 2 * BATCHES * TOKENS * D * D + 2 * BATCHES * TOKENS * D * KEYS
 
@@ -45,7 +45,7 @@ def tile_crossattention_pb_t_kernel(tc, text, Wq_w, Wq_b, qn_w, k_norm, out):
         ctx.enter_context(tc.manual_schedule())
         const = ctx.enter_context(tc.tile_pool(name="const", bufs=1))
         raw = ctx.enter_context(tc.tile_pool(name="raw", bufs=LOADS_AHEAD))
-        raw_keys = ctx.enter_context(tc.tile_pool(name="raw_keys", bufs=LOADS_AHEAD // BLOCKS_PER_BATCH))
+        raw_keys = ctx.enter_context(tc.tile_pool(name="raw_keys", bufs=LOADS_AHEAD))
         stage = ctx.enter_context(tc.tile_pool(name="stage", bufs=2))
         deep = ctx.enter_context(tc.tile_pool(name="deep", bufs=3))
         deeper = ctx.enter_context(tc.tile_pool(name="deeper", bufs=4))
@@ -65,23 +65,31 @@ def tile_crossattention_pb_t_kernel(tc, text, Wq_w, Wq_b, qn_w, k_norm, out):
         nc.scalar.dma_start(out=gain_bf[:], in_=qn_w.rearrange("(p c) -> p c", c=CHUNKS))
         live = {}
 
-        def load(n):
-            b, half = divmod(n, BLOCKS_PER_BATCH)
-            text_raw = raw.tile([P, BLOCK_TILES, D], BF16)
+        def load_text(b, tiles):
+            if ("raw", b) not in live:
+                text_raw = raw.tile([P, TILES_PER_BATCH, D], BF16)
+                live["raw", b] = text_raw
             nc.sync.dma_start(
-                out=text_raw[:],
-                in_=text[b].rearrange("(p i) k -> p i k", i=TILES_PER_BATCH)[
-                    :, half * BLOCK_TILES : (half + 1) * BLOCK_TILES, :
-                ],
+                out=live["raw", b][:, tiles, :],
+                in_=text[b].rearrange("(p i) k -> p i k", i=TILES_PER_BATCH)[:, tiles, :],
             )
-            live["text_raw", n] = text_raw
-            if half == 0:
-                k_raw = raw_keys.tile([P, KEY_TILES, D], BF16)
-                nc.sync.dma_start(out=k_raw[:], in_=k_norm[b].rearrange("(j p) d -> p j d", p=P))
-                live["k_raw", n] = k_raw
 
-        for n in range(LOADS_AHEAD):
-            load(n)
+        def load_keys(b):
+            k_raw = raw_keys.tile([P, KEY_TILES, D], BF16)
+            nc.sync.dma_start(out=k_raw[:], in_=k_norm[b].rearrange("(p j) d -> p j d", j=KEY_TILES))
+            live["k_raw", b] = k_raw
+
+        def load(b):
+            if 0 < b < BATCHES - 2:
+                load_text(b, slice(0, TILES_PER_BATCH))
+                load_keys(b)
+            else:
+                load_text(b, slice(0, BLOCK_TILES))
+                load_keys(b)
+                load_text(b, slice(BLOCK_TILES, TILES_PER_BATCH))
+
+        for b in range(LOADS_AHEAD):
+            load(b)
 
         ident = const.tile([P, P], F32)
         make_identity(nc, ident[:])
@@ -98,7 +106,7 @@ def tile_crossattention_pb_t_kernel(tc, text, Wq_w, Wq_b, qn_w, k_norm, out):
         k_codes = const.tile([P, BATCHES, KEYS], U32, align_bytes=64)
         k_scales = const.tile([P, BATCHES, KEYS], U8, align_bytes=64)
 
-        def turn(rows, n_tiles, copies, banks):
+        def turn(rows, n_tiles, copies, banks, interleave=False):
             words = rows.bitcast(F32)
             grouped = deep.tile([P, n_tiles * P, PACK], BF16, align_bytes=64, tag="grouped%d" % n_tiles)
             grouped_words = grouped[:].bitcast(F32)
@@ -109,10 +117,12 @@ def tile_crossattention_pb_t_kernel(tc, text, Wq_w, Wq_b, qn_w, k_norm, out):
                         nc.tensor.transpose(
                             turned[:, u, j * P : (j + 1) * P], words[:, first + j, u : 2 * P : 2], ident[:]
                         )
-                copy(
-                    out=grouped_words[:, first * P : (first + PAIR) * P, :],
-                    in_=turned[:].rearrange("p u r -> p r u"),
-                )
+                columns = grouped_words[:, first * P : (first + PAIR) * P, :]
+                turned_columns = turned[:].rearrange("p u r -> p r u")
+                if interleave:
+                    columns = columns.rearrange("p (q j) u -> p q j u", j=PAIR)
+                    turned_columns = turned[:].rearrange("p u (j q) -> p q j u", j=PAIR)
+                copy(out=columns, in_=turned_columns)
             return grouped
 
         turned_so_far = []
@@ -132,11 +142,14 @@ def tile_crossattention_pb_t_kernel(tc, text, Wq_w, Wq_b, qn_w, k_norm, out):
         def turn_text(n):
             copies = [nc.scalar.copy if n < FIRST else nc.vector.tensor_copy, nc.vector.tensor_copy]
             banks = next_banks(2) if n < FIRST else SCORE_BANKS
-            live["text", n] = turn(live["text_raw", n][:], BLOCK_TILES, copies, banks)
+            b, half = divmod(n, BLOCKS_PER_BATCH)
+            text_raw = live["raw", b][:, half * BLOCK_TILES : (half + 1) * BLOCK_TILES, :]
+            live["text", n] = turn(text_raw, BLOCK_TILES, copies, banks)
 
         def turn_keys(n):
             if n % BLOCKS_PER_BATCH == 0:
-                live["keys", n] = turn(live["k_raw", n][:], KEY_TILES, [nc.scalar.copy], next_banks(1))
+                k_raw = live["k_raw", n // BLOCKS_PER_BATCH]
+                live["keys", n] = turn(k_raw[:], KEY_TILES, [nc.scalar.copy], next_banks(1), interleave=True)
 
         def quantise_text(n):
             x_codes = ahead.tile([P, BLOCK], U32, align_bytes=64)
@@ -339,8 +352,9 @@ def tile_crossattention_pb_t_kernel(tc, text, Wq_w, Wq_b, qn_w, k_norm, out):
         for n in range(FIRST):
             turn_text(n)
             turn_keys(n)
-            if n + LOADS_AHEAD < N_BLOCKS:
-                load(n + LOADS_AHEAD)
+            b, half = divmod(n, BLOCKS_PER_BATCH)
+            if half == 1 and b + LOADS_AHEAD < BATCHES:
+                load(b + LOADS_AHEAD)
             if n == 0:
                 quantise(w_grouped, w_codes[:], w_scales[:])
                 nc.vector.tensor_copy(out=bias[:], in_=bias_bf[:])
@@ -370,8 +384,6 @@ def tile_crossattention_pb_t_kernel(tc, text, Wq_w, Wq_b, qn_w, k_norm, out):
             run(project, n + 1, (0, 1))
             if FIRST <= n + FIRST < N_BLOCKS:
                 turn_text(n + FIRST)
-                if n + FIRST + LOADS_AHEAD < N_BLOCKS:
-                    load(n + FIRST + LOADS_AHEAD)
                 quantise_text(n + FIRST)
             run(copy_spread, n - 1)
             run(normalise_on_gpsimd, n - 1)

from contextlib import ExitStack
import math

import concourse.mybir as mybir
from concourse.masks import make_identity

F32 = mybir.dt.float32
BF16 = mybir.dt.bfloat16
U32 = mybir.dt.uint32
U8 = mybir.dt.uint8
FP8X4 = mybir.dt.float8_e4m3fn_x4
ACT = mybir.ActivationFunctionType
ALU = mybir.AluOpType
AX = mybir.AxisListType

P = 128
PACK = 4
BATCHES = 8
TOKENS = 1024
KEYS = 256
D = 512
EPS = 1e-6

CHUNKS = D // P
TILES_PER_BATCH = TOKENS // P
KEY_TILES = KEYS // P
BLOCK_TILES = 4
BLOCK = BLOCK_TILES * P
BLOCKS_PER_BATCH = TOKENS // BLOCK
N_BLOCKS = BATCHES * BLOCKS_PER_BATCH
PAIR = 2
RUN = 4
Q_BANKS = ["q0", "q1", "q2", "q3"]
SCORE_BANKS = ["s0", "s1"]
FIRST = 15
SPLIT = 192
LOADS_AHEAD = 4

FLOPS = 2 * BATCHES * TOKENS * D * D + 2 * BATCHES * TOKENS * D * KEYS


def tile_crossattention_pb_t_kernel(tc, text, Wq_w, Wq_b, qn_w, k_norm, out):
    nc = tc.nc
    with ExitStack() as ctx:
        ctx.enter_context(tc.manual_schedule())
        const = ctx.enter_context(tc.tile_pool(name="const", bufs=1))
        raw = ctx.enter_context(tc.tile_pool(name="raw", bufs=LOADS_AHEAD))
        raw_keys = ctx.enter_context(tc.tile_pool(name="raw_keys", bufs=LOADS_AHEAD))
        stage = ctx.enter_context(tc.tile_pool(name="stage", bufs=2))
        deep = ctx.enter_context(tc.tile_pool(name="deep", bufs=3))
        deeper = ctx.enter_context(tc.tile_pool(name="deeper", bufs=4))
        ahead = ctx.enter_context(tc.tile_pool(name="ahead", bufs=N_BLOCKS))

        psum = ctx.enter_context(tc.psum_pool(name="psum", bufs=1))

        w_raw = const.tile([P, CHUNKS, D], BF16)
        for first in range(0, CHUNKS, PAIR):
            nc.sync.dma_start(
                out=w_raw[:, first : first + PAIR, :],
                in_=Wq_w.rearrange("(p c) k -> p c k", c=CHUNKS)[:, first : first + PAIR, :],
            )
        bias_bf = const.tile([P, CHUNKS], BF16)
        gain_bf = const.tile([P, CHUNKS], BF16)
        nc.scalar.dma_start(out=bias_bf[:], in_=Wq_b.rearrange("(p c) -> p c", c=CHUNKS))
        nc.scalar.dma_start(out=gain_bf[:], in_=qn_w.rearrange("(p c) -> p c", c=CHUNKS))
        live = {}

        def load_text(b, tiles):
            if ("raw", b) not in live:
                text_raw = raw.tile([P, TILES_PER_BATCH, D], BF16)
                live["raw", b] = text_raw
            nc.sync.dma_start(
                out=live["raw", b][:, tiles, :],
                in_=text[b].rearrange("(p i) k -> p i k", i=TILES_PER_BATCH)[:, tiles, :],
            )

        def load_keys(b):
            k_raw = raw_keys.tile([P, KEY_TILES, D], BF16)
            nc.sync.dma_start(out=k_raw[:], in_=k_norm[b].rearrange("(p j) d -> p j d", j=KEY_TILES))
            live["k_raw", b] = k_raw

        def load(b):
            if 0 < b < BATCHES - 2:
                load_text(b, slice(0, TILES_PER_BATCH))
                load_keys(b)
            else:
                load_text(b, slice(0, BLOCK_TILES))
                load_keys(b)
                load_text(b, slice(BLOCK_TILES, TILES_PER_BATCH))

        for b in range(LOADS_AHEAD):
            load(b)

        ident = const.tile([P, P], F32)
        make_identity(nc, ident[:])
        eps = const.tile([P, 1], F32)
        nc.vector.memset(eps[:], EPS)
        table = const.tile([P, 1], F32)
        nc.scalar.activation(out=table[:], in_=eps[:], func=ACT.Abs_reciprocal_sqrt, bias=eps[:], scale=1.0)
        bias = const.tile([P, CHUNKS], F32)
        gain = const.tile([P, CHUNKS], F32)
        gain_bias = const.tile([P, CHUNKS], F32)

        w_codes = const.tile([P, D], U32, align_bytes=64)
        w_scales = const.tile([P, D], U8, align_bytes=64)
        k_codes = const.tile([P, BATCHES, KEYS], U32, align_bytes=64)
        k_scales = const.tile([P, BATCHES, KEYS], U8, align_bytes=64)

        def turn(rows, n_tiles, copies, banks, interleave=False):
            words = rows.bitcast(F32)
            grouped = deep.tile([P, n_tiles * P, PACK], BF16, align_bytes=64, tag="grouped%d" % n_tiles)
            grouped_words = grouped[:].bitcast(F32)
            for copy, bank, first in zip(copies, banks, range(0, n_tiles, PAIR)):
                turned = psum.tile([P, 2, PAIR * P], F32, tag=bank)
                for j in range(PAIR):
                    for u in range(2):
                        nc.tensor.transpose(
                            turned[:, u, j * P : (j + 1) * P], words[:, first + j, u : 2 * P : 2], ident[:]
                        )
                columns = grouped_words[:, first * P : (first + PAIR) * P, :]
                turned_columns = turned[:].rearrange("p u r -> p r u")
                if interleave:
                    columns = columns.rearrange("p (q j) u -> p q j u", j=PAIR)
                    turned_columns = turned[:].rearrange("p u (j q) -> p q j u", j=PAIR)
                copy(out=columns, in_=turned_columns)
            return grouped

        turned_so_far = []

        def next_banks(count):
            banks = [(Q_BANKS + SCORE_BANKS)[(len(turned_so_far) + i) % 6] for i in range(count)]
            turned_so_far.extend(banks)
            return banks

        def quantise(grouped, codes, scales):
            nc.vector.quantize_mx(
                out=codes.bitcast(FP8X4), scales=scales, in_=grouped[:].rearrange("p r t -> p (r t)")
            )

        w_grouped = turn(w_raw[:], CHUNKS, [nc.scalar.copy, nc.vector.tensor_copy], next_banks(2))

        def turn_text(n):
            copies = [nc.scalar.copy if n < FIRST else nc.vector.tensor_copy, nc.vector.tensor_copy]
            banks = next_banks(2) if n < FIRST else SCORE_BANKS
            b, half = divmod(n, BLOCKS_PER_BATCH)
            text_raw = live["raw", b][:, half * BLOCK_TILES : (half + 1) * BLOCK_TILES, :]
            live["text", n] = turn(text_raw, BLOCK_TILES, copies, banks)

        def turn_keys(n):
            if n % BLOCKS_PER_BATCH == 0:
                k_raw = live["k_raw", n // BLOCKS_PER_BATCH]
                live["keys", n] = turn(k_raw[:], KEY_TILES, [nc.scalar.copy], next_banks(1), interleave=True)

        def quantise_text(n):
            x_codes = ahead.tile([P, BLOCK], U32, align_bytes=64)
            x_scales = ahead.tile([P, BLOCK], U8, align_bytes=64)
            quantise(live["text", n], x_codes[:], x_scales[:])
            live["x_mx", n] = (x_codes, x_scales)

        def quantise_keys(n):
            if n % BLOCKS_PER_BATCH == 0:
                b = n // BLOCKS_PER_BATCH
                quantise(live["keys", n], k_codes[:, b, :], k_scales[:, b, :])

        def project(n, chunks):
            x_codes, x_scales = live["x_mx", n]
            banks = live.setdefault(("q", n), [])
            for c in chunks:
                q_ps = psum.tile([P, BLOCK], F32, tag=Q_BANKS[c])
                nc.tensor.matmul_mx(
                    out=q_ps[:],
                    lhsT=w_codes[:, c * P : (c + 1) * P].bitcast(FP8X4),
                    lhsT_scale=w_scales[:, c * P : (c + 1) * P],
                    rhs=x_codes[:].bitcast(FP8X4),
                    rhs_scale=x_scales[:],
                    start=True,
                    stop=True,
                )
                banks.append(q_ps)

        def square(n, chunks=tuple(range(CHUNKS))):
            if 0 in chunks:
                squares = stage.tile([P, CHUNKS, BLOCK], F32)
                live["squares", n] = squares
            for c in chunks:
                nc.scalar.activation(
                    out=live["squares", n][:, c, :],
                    in_=live["q", n][c][:],
                    func=ACT.Square,
                    bias=bias[:, c : c + 1],
                    scale=1.0,
                )

        def add_pair(n):
            pair_sum = stage.tile([P, BLOCK], F32)
            squares = live["squares", n]
            nc.gpsimd.tensor_tensor(out=pair_sum[:], in0=squares[:, 0, :], in1=squares[:, 1, :], op=ALU.add)
            live["pair_sum", n] = pair_sum

        def scaled_tile(n):
            if ("scaled", n) not in live:
                scaled = deeper.tile([P, CHUNKS, BLOCK], F32)
                live["scaled", n] = scaled
            return live["scaled", n]

        def scale_on_vector(n, chunks):
            for c in chunks:
                cols = slice(0, SPLIT if c == 2 else BLOCK)
                nc.vector.tensor_scalar(
                    out=scaled_tile(n)[:, c, cols],
                    in0=live["q", n][c][:, cols],
                    scalar1=gain[:, c : c + 1],
                    scalar2=gain_bias[:, c : c + 1],
                    op0=ALU.mult,
                    op1=ALU.add,
                )

        def scale_on_scalar(n, chunks, split=SPLIT):
            for c in chunks:
                cols = slice(split if c == 2 else 0, BLOCK)
                nc.scalar.activation(
                    out=scaled_tile(n)[:, c, cols],
                    in_=live["q", n][c][:, cols],
                    func=ACT.Identity,
                    bias=gain_bias[:, c : c + 1],
                    scale=gain[:, c : c + 1],
                )

        def turn_squares(n):
            squares = live["squares", n]
            turned_sq = psum.tile([P, BLOCK_TILES, P], F32)
            for i in range(BLOCK_TILES):
                parts = [live["pair_sum", n][:], squares[:, 2, :], squares[:, 3, :]]
                for c, part in enumerate(parts):
                    nc.tensor.matmul(
                        out=turned_sq[:, i, :],
                        lhsT=part[:, i * P : (i + 1) * P],
                        rhs=ident[:],
                        start=(c == 0),
                        stop=(c == len(parts) - 1),
                        is_transpose=True,
                    )
            live["turned_sq", n] = turned_sq

        def sum_squares(n):
            sums = deep.tile([P, BLOCK_TILES], F32)
            nc.vector.tensor_reduce(out=sums[:], in_=live["turned_sq", n][:], axis=AX.X, op=ALU.add)
            live["sums", n] = sums

        def inverse_rms(n):
            rstd = deep.tile([P, BLOCK_TILES], F32)
            nc.scalar.activation(
                out=rstd[:], in_=live["sums", n][:], func=ACT.Abs_reciprocal_sqrt, bias=eps[:], scale=1.0 / D
            )
            live["rstd", n] = rstd

        def spread_inverse(n):
            spread = psum.tile([P, BLOCK], F32)
            for i in range(BLOCK_TILES):
                nc.tensor.transpose(
                    spread[:, i * P : (i + 1) * P], live["rstd", n][:, i : i + 1].to_broadcast([P, P]), ident[:]
                )
            live["spread", n] = spread

        def copy_spread(n):
            spread_copy = stage.tile([P, P], F32)
            nc.vector.tensor_copy(out=spread_copy[:], in_=live["spread", n][:, BLOCK - P :])
            live["spread_copy", n] = spread_copy

        def normalised_tile(n, pair):
            if ("normalised", n, pair) not in live:
                q_grouped = deep.tile([P, PAIR * P, PACK], BF16, align_bytes=64)
                live["normalised", n, pair] = q_grouped
            return live["normalised", n, pair]

        def normalise(engine, n, first, n_tiles, spread):
            pair, j = divmod(first, PAIR)
            tokens = n_tiles * P
            engine.tensor_tensor(
                out=normalised_tile(n, pair)[:, j * P : j * P + tokens, :].rearrange("p (t i) c -> p t c i", i=RUN),
                in0=live["scaled", n][:, :, first * P : first * P + tokens].rearrange("p c (t i) -> p t c i", i=RUN),
                in1=spread.rearrange("p (t i) -> p t i", i=RUN)
                .unsqueeze(2)
                .to_broadcast([P, tokens // RUN, PACK, RUN]),
                op=ALU.mult,
            )

        def normalise_on_vector(n, first, n_tiles):
            normalise(nc.vector, n, first, n_tiles, live["spread", n][:, first * P : (first + n_tiles) * P])

        def normalise_on_gpsimd(n):
            normalise(nc.gpsimd, n, BLOCK_TILES - 1, 1, live["spread_copy", n][:])

        def quantise_queries(n, pair):
            q_codes = deep.tile([P, PAIR * P], U32, align_bytes=64)
            q_scales = deep.tile([P, PAIR * P], U8, align_bytes=64)
            quantise(live["normalised", n, pair], q_codes[:], q_scales[:])
            live["q_mx", n, pair] = (q_codes, q_scales)

        def score(n, pair):
            b = n // BLOCKS_PER_BATCH
            q_codes, q_scales = live["q_mx", n, pair]
            s_ps = psum.tile([P, PAIR, KEYS], F32, tag=SCORE_BANKS[pair])
            for j in range(PAIR):
                nc.tensor.matmul_mx(
                    out=s_ps[:, j, :],
                    lhsT=q_codes[:, j * P : (j + 1) * P].bitcast(FP8X4),
                    lhsT_scale=q_scales[:, j * P : (j + 1) * P],
                    rhs=k_codes[:, b, :].bitcast(FP8X4),
                    rhs_scale=k_scales[:, b, :],
                    start=True,
                    stop=True,
                )
            live["s", n, pair] = s_ps

        def drain_on_vector(n, banks):
            for j in banks:
                nc.vector.tensor_scalar(
                    out=scores_tile(n)[:, j * PAIR : (j + 1) * PAIR, :],
                    in0=live["s", n, j][:],
                    scalar1=1.0 / math.sqrt(D),
                    scalar2=None,
                    op0=ALU.mult,
                )

        def drain_on_scalar(n, banks):
            for j in banks:
                nc.scalar.mul(
                    out=scores_tile(n)[:, j * PAIR : (j + 1) * PAIR, :], in_=live["s", n, j][:], mul=1.0 / math.sqrt(D)
                )

        def scores_tile(n):
            if ("scores", n) not in live:
                scores = deep.tile([P, BLOCK_TILES, KEYS], F32)
                live["scores", n] = scores
            return live["scores", n]

        def store(n, tiles=slice(0, BLOCK_TILES)):
            b, half = divmod(n, BLOCKS_PER_BATCH)
            first = half * BLOCK_TILES
            nc.sync.dma_start(
                out=out[b].rearrange("(p i) s -> p i s", i=TILES_PER_BATCH)[
                    :, first + tiles.start : first + tiles.stop, :
                ],
                in_=live["scores", n][:, tiles, :],
            )

        def run(stage_of_block, n, *more):
            if 0 <= n < N_BLOCKS:
                stage_of_block(n, *more)

        for n in range(FIRST):
            turn_text(n)
            turn_keys(n)
            b, half = divmod(n, BLOCKS_PER_BATCH)
            if half == 1 and b + LOADS_AHEAD < BATCHES:
                load(b + LOADS_AHEAD)
            if n == 0:
                quantise(w_grouped, w_codes[:], w_scales[:])
                nc.vector.tensor_copy(out=bias[:], in_=bias_bf[:])
                nc.vector.tensor_copy(out=gain[:], in_=gain_bf[:])
                nc.vector.tensor_tensor(out=gain_bias[:], in0=gain[:], in1=bias[:], op=ALU.mult)
            else:
                quantise_text(n - 1)
                quantise_keys(n - 1)
        quantise_text(FIRST - 1)
        quantise_keys(FIRST - 1)

        for n in range(-1, N_BLOCKS - 1):
            run(square, n, (0, 1))
            run(add_pair, n)
            run(project, n, (2, 3))
            run(quantise_queries, n - 2, 0)
            run(quantise_queries, n - 2, 1)
            run(score, n - 2, 0)
            run(score, n - 2, 1)
            run(sum_squares, n - 1)
            run(scale_on_scalar, n, (0,))
            run(inverse_rms, n - 1)
            run(scale_on_scalar, n, (1,))
            run(scale_on_vector, n, (2, 3))
            run(spread_inverse, n - 1)
            run(drain_on_vector, n - 2, (0,))
            run(project, n + 1, (0, 1))
            if FIRST <= n + FIRST < N_BLOCKS:
                turn_text(n + FIRST)
                quantise_text(n + FIRST)
            run(copy_spread, n - 1)
            run(normalise_on_gpsimd, n - 1)
            run(normalise_on_vector, n - 1, 0, 2)
            run(square, n, (2, 3))
            run(turn_squares, n)
            run(scale_on_scalar, n, (2,))
            run(normalise_on_vector, n - 1, 2, 1)
            run(drain_on_scalar, n - 2, (1,))
            run(store, n - 2)

        last = N_BLOCKS - 1
        square(last, (0, 1))
        add_pair(last)
        project(last, (2, 3))
        quantise_queries(last - 2, 0)
        quantise_queries(last - 2, 1)
        score(last - 2, 0)
        sum_squares(last - 1)
        square(last, (2,))
        inverse_rms(last - 1)
        square(last, (3,))
        spread_inverse(last - 1)
        score(last - 2, 1)
        drain_on_vector(last - 2, (0,))
        copy_spread(last - 1)
        normalise_on_gpsimd(last - 1)
        turn_squares(last)
        normalise_on_vector(last - 1, 0, 2)
        scale_on_scalar(last, (0, 1, 2, 3), 0)
        sum_squares(last)
        normalise_on_vector(last - 1, 2, 1)
        inverse_rms(last)
        drain_on_scalar(last - 2, (1,))
        store(last - 2)
        quantise_queries(last - 1, 0)
        quantise_queries(last - 1, 1)
        spread_inverse(last)
        score(last - 1, 0)
        score(last - 1, 1)
        copy_spread(last)
        normalise_on_gpsimd(last)
        drain_on_scalar(last - 1, (0, 1))
        store(last - 1)
        normalise_on_vector(last, 0, 2)
        normalise_on_vector(last, 2, 1)
        quantise_queries(last, 0)
        quantise_queries(last, 1)
        score(last, 0)
        score(last, 1)
        drain_on_vector(last, (0,))
        store(last, slice(0, PAIR))
        drain_on_scalar(last, (1,))
        store(last, slice(PAIR, BLOCK_TILES))
